import numpy as np
import ml_dtypes


def mxq(x, axis, fmt="e4m3"):
    dtype, down = {"e4m3": (ml_dtypes.float8_e4m3fn, 7), "e5m2": (ml_dtypes.float8_e5m2, 14)}[fmt]
    v = np.moveaxis(np.asarray(x, np.float32).astype(ml_dtypes.bfloat16).astype(np.float64), axis, -1)
    blocks = v.reshape(v.shape[:-1] + (-1, 32))
    amax = np.abs(blocks).max(-1, keepdims=True)
    byte = np.maximum(np.where(amax > 0, np.frexp(amax)[1] - 1 + 127, 0) - down, 1)
    scale = np.exp2(byte - 127.0)
    codes = (blocks / scale).astype(np.float32).astype(dtype).astype(np.float64)
    return np.moveaxis((codes * scale).reshape(v.shape), -1, axis)


WIDE = False


def mx_kscale(k):
    if not WIDE:
        return np.ones(k)
    levels = np.array([10, -10, 5, -5, 0])
    a = np.random.permutation(np.resize(levels, k // 512 * 4)).reshape(k // 512, 4)
    idx = np.arange(k)
    return np.exp2(a[idx // 512, idx % 128 // 32])


BF16 = ml_dtypes.bfloat16


def bf(x):
    return np.asarray(x, np.float32).astype(BF16)


def f64(x):
    return np.asarray(x).astype(np.float64)


E2M1 = np.array([0.0, 0.5, 1.0, 1.5, 2.0, 3.0, 4.0, 6.0, -0.0, -0.5, -1.0, -1.5, -2.0, -3.0, -4.0, -6.0])


def pack_weight(w, fmt):
    k, n = w.shape
    w = f64(bf(w)).reshape(k // 32, 32, n)
    amax = np.abs(w).max(1)
    if fmt == "e4m3":
        byte = np.frexp(amax)[1] - 1 + 127 - 7
    else:
        mant, ex = np.frexp(amax / 6.0)
        byte = np.where(mant > 0.5, ex, ex - 1) + 127
    byte = np.clip(np.where(amax > 0, byte, 1), 1, 254)
    scaled = (w * np.exp2(127.0 - byte)[:, None, :]).reshape(k, n).astype(np.float32)
    by_word = np.ascontiguousarray(scaled.reshape(k // 512, 128, 4, n).transpose(0, 1, 3, 2))
    if fmt == "e4m3":
        words = by_word.astype(ml_dtypes.float8_e4m3fn).view(np.uint8)
    else:
        c = by_word.astype(ml_dtypes.float4_e2m1fn).view(np.uint8) & 0xF
        words = c[..., 0::2] | (c[..., 1::2] << 4)
    return np.ascontiguousarray(words), np.ascontiguousarray(byte.astype(np.uint8).reshape(k // 512, 16, n))


def unpack_weight(words, scales, fmt):
    g, p, n, _ = words.shape
    if fmt == "e4m3":
        vals = np.ascontiguousarray(words).view(ml_dtypes.float8_e4m3fn).astype(np.float64)
    else:
        nib = np.empty((g, p, n, 4), np.uint8)
        nib[..., 0::2] = words & 0xF
        nib[..., 1::2] = words >> 4
        vals = E2M1[nib]
    vals = vals * np.repeat(np.exp2(scales.astype(np.float64) - 127.0), 8, axis=1)[..., None]
    return vals.transpose(0, 1, 3, 2).reshape(g * 512, n)


B, DI, DH = 256, 16384, 128


def sigmoid(v):
    return 1.0 / (1.0 + np.exp(-v))


def setup_inputs():
    s = mx_kscale(DI)
    n = np.random.standard_normal
    a, c = 0.7 / np.sqrt(DI), 0.7 / np.sqrt(DH)
    keep = np.random.uniform(size=B) < 0.9
    out = {
        "x": bf(n((B, DI)) * s),
        "h_minors": bf(n((B, DH))),
        "c_minors": bf(n((B, DH))),
        "s0": bf(n((B, DH))),
        "s1": bf(n((B, DH))),
        "s2": bf(n((B, DH))),
        "mask": bf(keep * (0.5 + 0.5 * np.random.uniform(size=B))),
    }
    words, scales = pack_weight((n((7 * DH, DI)) * a / s).T, "e4m3")
    out["weight_ih_words"] = words
    out["weight_ih_scales"] = scales
    out.update({
        "bias_ih": bf(n(7 * DH) * 0.3),
        "weight_hh": bf(n((4 * DH, DH)) * c),
        "bias_hh": bf(n(4 * DH) * 0.3),
        "weight_sh0": bf(n((DH, DH)) * c),
        "bias_sh0": bf(n(DH) * 0.3),
        "weight_sh1": bf(n((DH, DH)) * c),
        "bias_sh1": bf(n(DH) * 0.3),
        "weight_sh2": bf(n((DH, DH)) * c),
        "bias_sh2": bf(n(DH) * 0.3),
    })
    return out


def reference(x, h_minors, c_minors, s0, s1, s2, mask, weight_ih_words, weight_ih_scales, bias_ih, weight_hh, bias_hh,
              weight_sh0, bias_sh0, weight_sh1, bias_sh1, weight_sh2, bias_sh2):
    d = DH
    m = f64(mask)[:, None]

    tmp = (mxq(f64(x), 1, "e4m3") @ unpack_weight(weight_ih_words, weight_ih_scales, "e4m3")) + f64(bias_ih)
    tmp2 = f64(h_minors) @ f64(weight_hh).T + f64(bias_hh)
    tmp3 = np.concatenate([
        f64(s0) @ f64(weight_sh0).T + f64(bias_sh0),
        f64(s1) @ f64(weight_sh1).T + f64(bias_sh1),
        f64(s2) @ f64(weight_sh2).T + f64(bias_sh2),
    ], axis=1)

    tmp_in, tmp_s = tmp[:, :4 * d], tmp[:, 4 * d:]
    pre = tmp_in + tmp2
    ifo = sigmoid(pre[:, :3 * d])
    c_hat = pre[:, 3 * d:]
    i_g, f_g, o_g = ifo[:, :d], ifo[:, d:2 * d], ifo[:, 2 * d:]

    c_t = (f_g * f64(c_minors) + i_g * np.tanh(c_hat)) * m
    tc = np.tanh(c_t) * m
    h = o_g * tc

    bg = sigmoid(tmp_s + tmp3)
    b0, b1, b2 = bg[:, :d], bg[:, d:2 * d], bg[:, 2 * d:]

    s_0 = (b0 + 1.0 - o_g) * tc
    s_1 = (b1 + 2.0 - o_g - s_0) * 0.5 * tc
    s_2 = (b2 + 3.0 - o_g - (2.0 * s_0 + s_1)) * (1.0 / 3.0) * tc

    return (h, c_t, s_0, s_1, s_2)

@@ -1,0 +1,302 @@
+from contextlib import ExitStack
+
+import concourse.mybir as mybir
+from concourse.masks import make_identity
+
+F32 = mybir.dt.float32
+BF16 = mybir.dt.bfloat16
+I32 = mybir.dt.int32
+U32 = mybir.dt.uint32
+U8 = mybir.dt.uint8
+FP8X4 = mybir.dt.float8_e4m3fn_x4
+ALU = mybir.AluOpType
+ACT = mybir.ActivationFunctionType
+
+P = 128
+HALVES = 2
+DH = 128
+K_PASS = 512
+WORDS = K_PASS // 2
+GROUPS = 16384 // K_PASS
+N_ALL = 7 * DH
+N_LSTM = 4 * DH
+
+ROUND = 2
+ROUNDS = GROUPS // ROUND
+BLOCK = 4
+BLOCKS = GROUPS // BLOCK
+ROUNDS_IN_BLOCK = BLOCK // ROUND
+AHEAD = 3
+
+COLUMN_RANGES = ((0, 512), (512, 256), (768, 128))
+
+FLOPS = 2 * 256 * 16384 * N_ALL + 2 * 256 * DH * N_ALL
+
+
+def tile_share_lstm_cell_pa_k_kernel(
+    tc,
+    x,
+    h_minors,
+    c_minors,
+    s0,
+    s1,
+    s2,
+    mask,
+    weight_ih_words,
+    weight_ih_scales,
+    bias_ih,
+    weight_hh,
+    bias_hh,
+    weight_sh0,
+    bias_sh0,
+    weight_sh1,
+    bias_sh1,
+    weight_sh2,
+    bias_sh2,
+    out_0,
+    out_1,
+    out_2,
+    out_3,
+    out_4,
+):
+    nc = tc.nc
+    x_rows = x.rearrange("(p h) k -> p h k", h=HALVES)
+    w_words = weight_ih_words.rearrange("g p n t -> p g (n t)")
+
+    with ExitStack() as ctx:
+        ctx.enter_context(tc.manual_schedule())
+        keep = ctx.enter_context(tc.tile_pool(name="keep", bufs=1))
+        x_pool = ctx.enter_context(tc.tile_pool(name="x_pool", bufs=AHEAD + 1))
+        w_pool = ctx.enter_context(tc.tile_pool(name="w_pool", bufs=ROUNDS_IN_BLOCK * (AHEAD + 1)))
+        sort_pool = ctx.enter_context(tc.tile_pool(name="sort_pool", bufs=2))
+        quant_pool = ctx.enter_context(tc.tile_pool(name="quant_pool", bufs=3))
+        acc_pool = ctx.enter_context(tc.psum_pool(name="acc_pool", bufs=1))
+        flip_pool = ctx.enter_context(tc.psum_pool(name="flip_pool", bufs=ROUND))
+
+        w_planes = keep.tile([P, BLOCKS, N_ALL], U8, align_bytes=64)
+
+        x_tiles = {}
+        w_tiles = {}
+
+        def load_x(block):
+            x_tile = x_pool.tile([P, HALVES, BLOCK * K_PASS], BF16, name="x_tile")
+            k_from = block * BLOCK * K_PASS
+            nc.sync.dma_start(out=x_tile[:], in_=x_rows[:, :, k_from : k_from + BLOCK * K_PASS])
+            x_tiles[block] = x_tile
+
+        def load_w(rnd):
+            w_tile = w_pool.tile([P, ROUND, N_ALL], U32, name="w_tile", align_bytes=64)
+            nc.sync.dma_start(
+                out=w_tile[:].bitcast(I32),
+                in_=w_words[:, rnd * ROUND : (rnd + 1) * ROUND, :].bitcast(I32),
+            )
+            w_tiles[rnd] = w_tile
+
+        def load_block(block):
+            for quadrant in range(4):
+                nc.sync.dma_start(
+                    out=w_planes[32 * quadrant : 32 * quadrant + 16, block, :].bitcast(I32),
+                    in_=weight_ih_scales[
+                        block * BLOCK : (block + 1) * BLOCK, 4 * quadrant : 4 * quadrant + 4, :
+                    ].bitcast(I32),
+                )
+            load_w(block * ROUNDS_IN_BLOCK)
+            if block + 1 < BLOCKS:
+                load_x(block + 1)
+            load_w(block * ROUNDS_IN_BLOCK + 1)
+
+        acts_in = keep.tile([P, 4, HALVES, DH], BF16)
+        for a, rows in enumerate((h_minors, s0, s1, s2)):
+            nc.sync.dma_start(out=acts_in[:, a], in_=rows.rearrange("(p h) k -> p h k", h=HALVES))
+        wts_in = keep.tile([P, 7, DH], BF16)
+        nc.sync.dma_start(out=wts_in[:, 0:4, :], in_=weight_hh.rearrange("(j n) k -> n j k", j=4))
+        for j, rows in enumerate((weight_sh0, weight_sh1, weight_sh2)):
+            nc.sync.dma_start(out=wts_in[:, 4 + j, :], in_=rows)
+        bias_rows = keep.tile([P, N_ALL], BF16)
+        nc.vector.memset(bias_rows[:], 0.0)
+        nc.sync.dma_start(out=bias_rows[0:1, :], in_=bias_ih.unsqueeze(0))
+        nc.sync.dma_start(out=bias_rows[1:2, 0:N_LSTM], in_=bias_hh.unsqueeze(0))
+        for j, row in enumerate((bias_sh0, bias_sh1, bias_sh2)):
+            nc.sync.dma_start(
+                out=bias_rows[1:2, N_LSTM + j * DH : N_LSTM + (j + 1) * DH], in_=row.unsqueeze(0)
+            )
+        nc.vector.memset(w_planes[:].bitcast(I32), 0)
+        load_x(0)
+        for block in range(AHEAD):
+            load_block(block)
+        c_in = keep.tile([P, HALVES, DH], BF16)
+        nc.sync.dma_start(out=c_in[:], in_=c_minors.rearrange("(p h) k -> p h k", h=HALVES))
+        mask_in = keep.tile([P, HALVES], BF16)
+        nc.sync.dma_start(out=mask_in[:], in_=mask.rearrange("(p h) -> p h", h=HALVES))
+
+        ident_bf16 = keep.tile([P, P], BF16)
+        make_identity(nc, ident_bf16[:])
+        ident_f32 = keep.tile([P, P], F32)
+        make_identity(nc, ident_f32[:])
+        ones = keep.tile([P, P], BF16)
+        nc.gpsimd.memset(ones[:], 1.0)
+        warm = keep.tile([P, 1], F32)
+        nc.vector.memset(warm[:], 0.0)
+        nc.scalar.activation(out=warm[:], in_=warm[:], func=ACT.Sigmoid)
+
+        sorted_blocks = {}
+        x_codes = {}
+        x_planes = {}
+
+        def sort_x(block):
+            sorted_block = sort_pool.tile([P, HALVES, BLOCK, 2, P], F32, name="sorted_block")
+            nc.vector.tensor_copy(
+                out=sorted_block[:],
+                in_=x_tiles[block][:].bitcast(F32).rearrange("p h (g w u) -> p h g u w", g=BLOCK, u=2),
+            )
+            sorted_blocks[block] = sorted_block
+
+        def flip_x(rnd):
+            block, part = divmod(rnd, ROUNDS_IN_BLOCK)
+            grouped = quant_pool.tile([P, ROUND * HALVES * P * 4], BF16, name="grouped", align_bytes=64)
+            grouped_words = grouped[:].bitcast(F32).rearrange("p (g c u) -> p g c u", g=ROUND, u=2)
+            for g in range(ROUND):
+                flipped = flip_pool.tile([P, 2, HALVES, P], F32, name="flipped")
+                for u in range(2):
+                    for h in range(HALVES):
+                        nc.tensor.transpose(
+                            flipped[:, u, h, :],
+                            sorted_blocks[block][:, h, part * ROUND + g, u, :],
+                            ident_f32[:],
+                        )
+                nc.scalar.copy(out=grouped_words[:, g], in_=flipped[:].rearrange("p u h b -> p (h b) u"))
+            codes = quant_pool.tile([P, ROUND * HALVES * P], U32, name="codes", align_bytes=64)
+            plane = quant_pool.tile([P, ROUND * HALVES * P], U8, name="plane", align_bytes=64)
+            nc.vector.quantize_mx(out=codes[:].bitcast(FP8X4), scales=plane[:], in_=grouped[:])
+            x_codes[rnd] = codes
+            x_planes[rnd] = plane
+
+        acts_flip = acc_pool.tile([P, 4 * HALVES, P], BF16, tag="acc_2_0")
+        for a in range(4):
+            for h in range(HALVES):
+                nc.tensor.transpose(acts_flip[:, a * HALVES + h, :], acts_in[:, a, h, :], ident_bf16[:])
+        acts_t = keep.tile([P, 4 * HALVES, P], BF16)
+        nc.scalar.copy(out=acts_t[:], in_=acts_flip[:])
+        wts_flip = acc_pool.tile([P, 7, P], BF16, tag="acc_2_1")
+        for j in range(7):
+            nc.tensor.transpose(wts_flip[:, j, :], wts_in[:, j, :], ident_bf16[:])
+        wts_t = keep.tile([P, N_ALL], BF16)
+        nc.scalar.copy(out=wts_t[:], in_=wts_flip[:].rearrange("p j n -> p (j n)"))
+
+        addend = keep.tile([P, HALVES, N_ALL], F32)
+        for h in range(HALVES):
+            lstm_sum = acc_pool.tile([P, N_LSTM], F32, tag="acc_0_%d" % h)
+            nc.tensor.matmul(lstm_sum[:], lhsT=ones[:], rhs=bias_rows[:, 0:N_LSTM], start=True, stop=False)
+            nc.tensor.matmul(lstm_sum[:], lhsT=acts_t[:, h, :], rhs=wts_t[:, 0:N_LSTM], start=False, stop=True)
+            nc.scalar.copy(out=addend[:, h, 0:N_LSTM], in_=lstm_sum[:])
+            shared_sum = acc_pool.tile([P, 3 * DH], F32, tag="acc_1_%d" % h)
+            for j in range(3):
+                cols = slice(N_LSTM + j * DH, N_LSTM + (j + 1) * DH)
+                part_sum = shared_sum[:, j * DH : (j + 1) * DH]
+                nc.tensor.matmul(part_sum, lhsT=ones[:], rhs=bias_rows[:, cols], start=True, stop=False)
+                nc.tensor.matmul(
+                    part_sum, lhsT=acts_t[:, (1 + j) * HALVES + h, :], rhs=wts_t[:, cols], start=False, stop=True
+                )
+            nc.scalar.copy(out=addend[:, h, N_LSTM:N_ALL], in_=shared_sum[:])
+
+        acc = {}
+        for c, (col_from, width) in enumerate(COLUMN_RANGES):
+            for h in range(HALVES):
+                acc[c, h] = acc_pool.tile([P, width], F32, name="acc", tag="acc_%d_%d" % (c, h))
+
+        sort_x(0)
+        flip_x(0)
+        for rnd in range(ROUNDS):
+            block, part = divmod(rnd, ROUNDS_IN_BLOCK)
+            if part == 0 and block + AHEAD < BLOCKS:
+                load_block(block + AHEAD)
+            if part == 0 and block + 1 < BLOCKS:
+                sort_x(block + 1)
+            if rnd + 1 < ROUNDS:
+                flip_x(rnd + 1)
+            for c, (col_from, width) in enumerate(COLUMN_RANGES):
+                for h in range(HALVES):
+                    for g in range(ROUND):
+                        offset = 4 * (part * ROUND + g)
+                        rows = slice((g * HALVES + h) * P, (g * HALVES + h + 1) * P)
+                        nc.tensor.matmul_mx(
+                            out=acc[c, h][:],
+                            lhsT=x_codes[rnd][:, rows].bitcast(FP8X4),
+                            lhsT_scale=x_planes[rnd][:, rows],
+                            rhs=w_tiles[rnd][:, g, col_from : col_from + width].bitcast(FP8X4),
+                            rhs_scale=w_planes[offset:P, block, col_from : col_from + width],
+                            start=(rnd == 0 and g == 0),
+                            stop=(rnd == ROUNDS - 1 and g == ROUND - 1),
+                        )
+
+        mask_col = keep.tile([P, HALVES], F32)
+        nc.scalar.copy(out=mask_col[:], in_=mask_in[:])
+        pre = keep.tile([P, HALVES, N_ALL], F32)
+        gate = keep.tile([P, HALVES, N_ALL], F32)
+        for c, (col_from, width) in enumerate(COLUMN_RANGES):
+            for h in range(HALVES):
+                cols = slice(col_from, col_from + width)
+                nc.vector.tensor_tensor(out=pre[:, h, cols], in0=acc[c, h][:], in1=addend[:, h, cols], op=ALU.add)
+        for h in range(HALVES):
+            nc.scalar.activation(out=gate[:, h, 0 : 3 * DH], in_=pre[:, h, 0 : 3 * DH], func=ACT.Sigmoid)
+            nc.scalar.activation(out=gate[:, h, 3 * DH : N_LSTM], in_=pre[:, h, 3 * DH : N_LSTM], func=ACT.Tanh)
+        for h in range(HALVES):
+            nc.scalar.activation(out=gate[:, h, N_LSTM:N_ALL], in_=pre[:, h, N_LSTM:N_ALL], func=ACT.Sigmoid)
+        i_gate = gate[:, :, 0:DH]
+        f_gate = gate[:, :, DH : 2 * DH]
+        o_gate = gate[:, :, 2 * DH : 3 * DH]
+        c_hat = gate[:, :, 3 * DH : 4 * DH]
+        mask_wide = mask_col[:].unsqueeze(2).to_broadcast([P, HALVES, DH])
+
+        def result(name):
+            return keep.tile([P, HALVES, DH], F32, name=name)
+
+        def store(out, tile):
+            nc.sync.dma_start(out=out.rearrange("(p h) n -> p h n", h=HALVES), in_=tile[:])
+
+        kept = result("kept")
+        nc.vector.tensor_tensor(out=kept[:], in0=f_gate, in1=c_in[:], op=ALU.mult)
+        fresh = result("fresh")
+        nc.vector.tensor_tensor(out=fresh[:], in0=i_gate, in1=c_hat, op=ALU.mult)
+        cell = result("cell")
+        nc.vector.tensor_tensor(out=cell[:], in0=kept[:], in1=fresh[:], op=ALU.add)
+        tanh_c = result("tanh_c")
+        for h in range(HALVES):
+            nc.scalar.activation(out=tanh_c[:, h, :], in_=cell[:, h, :], func=ACT.Tanh, scale=mask_col[:, h : h + 1])
+        c_t = result("c_t")
+        nc.vector.tensor_tensor(out=c_t[:], in0=cell[:], in1=mask_wide, op=ALU.mult)
+        store(out_1, c_t)
+        lead = [result("lead%d" % j) for j in range(3)]
+        for j in range(3):
+            nc.vector.scalar_tensor_tensor(
+                out=lead[j][:],
+                in0=gate[:, :, N_LSTM + j * DH : N_LSTM + (j + 1) * DH],
+                scalar=float(j + 1),
+                in1=o_gate,
+                op0=ALU.add,
+                op1=ALU.subtract,
+            )
+        t = result("t")
+        nc.vector.scalar_tensor_tensor(out=t[:], in0=tanh_c[:], scalar=0.0, in1=mask_wide, op0=ALU.add, op1=ALU.mult)
+        h_out = result("h_out")
+        nc.vector.tensor_tensor(out=h_out[:], in0=o_gate, in1=t[:], op=ALU.mult)
+        store(out_0, h_out)
+        s_0 = result("s_0")
+        nc.vector.tensor_tensor(out=s_0[:], in0=lead[0][:], in1=t[:], op=ALU.mult)
+        store(out_2, s_0)
+        rest_1 = result("rest_1")
+        nc.vector.tensor_tensor(out=rest_1[:], in0=lead[1][:], in1=s_0[:], op=ALU.subtract)
+        s_1 = result("s_1")
+        nc.vector.scalar_tensor_tensor(out=s_1[:], in0=rest_1[:], scalar=0.5, in1=t[:], op0=ALU.mult, op1=ALU.mult)
+        store(out_3, s_1)
+        rest_2a = result("rest_2a")
+        nc.vector.scalar_tensor_tensor(
+            out=rest_2a[:], in0=s_0[:], scalar=-2.0, in1=lead[2][:], op0=ALU.mult, op1=ALU.add
+        )
+        rest_2 = result("rest_2")
+        nc.vector.tensor_tensor(out=rest_2[:], in0=rest_2a[:], in1=s_1[:], op=ALU.subtract)
+        s_2 = result("s_2")
+        nc.vector.scalar_tensor_tensor(
+            out=s_2[:], in0=rest_2[:], scalar=1.0 / 3.0, in1=t[:], op0=ALU.mult, op1=ALU.mult
+        )
+        store(out_4, s_2)

@@ -93,13 +93,6 @@ def tile_share_lstm_cell_pa_k_kernel(
             w_tiles[rnd] = w_tile
 
         def load_block(block):
-            for quadrant in range(4):
-                nc.sync.dma_start(
-                    out=w_planes[32 * quadrant : 32 * quadrant + 16, block, :].bitcast(I32),
-                    in_=weight_ih_scales[
-                        block * BLOCK : (block + 1) * BLOCK, 4 * quadrant : 4 * quadrant + 4, :
-                    ].bitcast(I32),
-                )
             load_w(block * ROUNDS_IN_BLOCK)
             if block + 1 < BLOCKS:
                 load_x(block + 1)
@@ -135,6 +128,14 @@ def tile_share_lstm_cell_pa_k_kernel(
         make_identity(nc, ident_f32[:])
         ones = keep.tile([P, P], BF16)
         nc.gpsimd.memset(ones[:], 1.0)
+        for block in range(BLOCKS):
+            for quadrant in range(4):
+                nc.gpsimd.dma_start(
+                    out=w_planes[32 * quadrant : 32 * quadrant + 16, block, :].bitcast(F32),
+                    in_=weight_ih_scales[
+                        block * BLOCK : (block + 1) * BLOCK, 4 * quadrant : 4 * quadrant + 4, :
+                    ].bitcast(F32),
+                )
         warm = keep.tile([P, 1], F32)
         nc.vector.memset(warm[:], 0.0)
         nc.scalar.activation(out=warm[:], in_=warm[:], func=ACT.Sigmoid)

@@ -103,18 +103,18 @@ def tile_share_lstm_cell_pa_k_kernel(
             nc.sync.dma_start(out=acts_in[:, a], in_=rows.rearrange("(p h) k -> p h k", h=HALVES))
         wts_in = keep.tile([P, 7, DH], BF16)
         nc.sync.dma_start(out=wts_in[:, 0:4, :], in_=weight_hh.rearrange("(j n) k -> n j k", j=4))
-        for j, rows in enumerate((weight_sh0, weight_sh1, weight_sh2)):
-            nc.sync.dma_start(out=wts_in[:, 4 + j, :], in_=rows)
         bias_rows = keep.tile([P, N_ALL], BF16)
         nc.vector.memset(bias_rows[:], 0.0)
         nc.sync.dma_start(out=bias_rows[0:1, :], in_=bias_ih.unsqueeze(0))
         nc.sync.dma_start(out=bias_rows[1:2, 0:N_LSTM], in_=bias_hh.unsqueeze(0))
+        load_x(0)
+        for j, rows in enumerate((weight_sh0, weight_sh1, weight_sh2)):
+            nc.sync.dma_start(out=wts_in[:, 4 + j, :], in_=rows)
         for j, row in enumerate((bias_sh0, bias_sh1, bias_sh2)):
             nc.sync.dma_start(
                 out=bias_rows[1:2, N_LSTM + j * DH : N_LSTM + (j + 1) * DH], in_=row.unsqueeze(0)
             )
         nc.vector.memset(w_planes[:].bitcast(I32), 0)
-        load_x(0)
         for block in range(AHEAD):
             load_block(block)
         c_in = keep.tile([P, HALVES, DH], BF16)
@@ -179,10 +179,10 @@ def tile_share_lstm_cell_pa_k_kernel(
         acts_t = keep.tile([P, 4 * HALVES, P], BF16)
         nc.scalar.copy(out=acts_t[:], in_=acts_flip[:])
         wts_flip = acc_pool.tile([P, 7, P], BF16, tag="acc_2_1")
-        for j in range(7):
-            nc.tensor.transpose(wts_flip[:, j, :], wts_in[:, j, :], ident_bf16[:])
         wts_t = keep.tile([P, N_ALL], BF16)
-        nc.scalar.copy(out=wts_t[:], in_=wts_flip[:].rearrange("p j n -> p (j n)"))
+        for j in range(4):
+            nc.tensor.transpose(wts_flip[:, j, :], wts_in[:, j, :], ident_bf16[:])
+        nc.scalar.copy(out=wts_t[:, 0:N_LSTM], in_=wts_flip[:, 0:4, :].rearrange("p j n -> p (j n)"))
 
         addend = keep.tile([P, HALVES, N_ALL], F32)
         for h in range(HALVES):
@@ -190,6 +190,10 @@ def tile_share_lstm_cell_pa_k_kernel(
             nc.tensor.matmul(lstm_sum[:], lhsT=ones[:], rhs=bias_rows[:, 0:N_LSTM], start=True, stop=False)
             nc.tensor.matmul(lstm_sum[:], lhsT=acts_t[:, h, :], rhs=wts_t[:, 0:N_LSTM], start=False, stop=True)
             nc.scalar.copy(out=addend[:, h, 0:N_LSTM], in_=lstm_sum[:])
+        for j in range(4, 7):
+            nc.tensor.transpose(wts_flip[:, j, :], wts_in[:, j, :], ident_bf16[:])
+        nc.scalar.copy(out=wts_t[:, N_LSTM:N_ALL], in_=wts_flip[:, 4:7, :].rearrange("p j n -> p (j n)"))
+        for h in range(HALVES):
             shared_sum = acc_pool.tile([P, 3 * DH], F32, tag="acc_1_%d" % h)
             for j in range(3):
                 cols = slice(N_LSTM + j * DH, N_LSTM + (j + 1) * DH)
@@ -230,8 +234,18 @@ def tile_share_lstm_cell_pa_k_kernel(
                             stop=(rnd == ROUNDS - 1 and g == ROUND - 1),
                         )
 
+        def result(name):
+            return keep.tile([P, HALVES, DH], F32, name=name)
+
+        def store(out, tile):
+            nc.sync.dma_start(out=out.rearrange("(p h) n -> p h n", h=HALVES), in_=tile[:])
+
         mask_col = keep.tile([P, HALVES], F32)
         nc.scalar.copy(out=mask_col[:], in_=mask_in[:])
+        mask_wide = mask_col[:].unsqueeze(2).to_broadcast([P, HALVES, DH])
+        c_masked = result("c_masked")
+        nc.vector.tensor_tensor(out=c_masked[:], in0=c_in[:], in1=mask_wide, op=ALU.mult)
+
         pre = keep.tile([P, HALVES, N_ALL], F32)
         gate = keep.tile([P, HALVES, N_ALL], F32)
         for c, (col_from, width) in enumerate(COLUMN_RANGES):
@@ -247,53 +261,56 @@ def tile_share_lstm_cell_pa_k_kernel(
         f_gate = gate[:, :, DH : 2 * DH]
         o_gate = gate[:, :, 2 * DH : 3 * DH]
         c_hat = gate[:, :, 3 * DH : 4 * DH]
-        mask_wide = mask_col[:].unsqueeze(2).to_broadcast([P, HALVES, DH])
 
-        def result(name):
-            return keep.tile([P, HALVES, DH], F32, name=name)
-
-        def store(out, tile):
-            nc.sync.dma_start(out=out.rearrange("(p h) n -> p h n", h=HALVES), in_=tile[:])
-
-        kept = result("kept")
-        nc.vector.tensor_tensor(out=kept[:], in0=f_gate, in1=c_in[:], op=ALU.mult)
-        fresh = result("fresh")
-        nc.vector.tensor_tensor(out=fresh[:], in0=i_gate, in1=c_hat, op=ALU.mult)
-        cell = result("cell")
-        nc.vector.tensor_tensor(out=cell[:], in0=kept[:], in1=fresh[:], op=ALU.add)
-        tanh_c = result("tanh_c")
-        for h in range(HALVES):
-            nc.scalar.activation(out=tanh_c[:, h, :], in_=cell[:, h, :], func=ACT.Tanh, scale=mask_col[:, h : h + 1])
-        c_t = result("c_t")
-        nc.vector.tensor_tensor(out=c_t[:], in0=cell[:], in1=mask_wide, op=ALU.mult)
-        store(out_1, c_t)
-        lead = [result("lead%d" % j) for j in range(3)]
-        for j in range(3):
+        def lead(j):
+            lead_j = result("lead%d" % j)
             nc.vector.scalar_tensor_tensor(
-                out=lead[j][:],
+                out=lead_j[:],
                 in0=gate[:, :, N_LSTM + j * DH : N_LSTM + (j + 1) * DH],
                 scalar=float(j + 1),
                 in1=o_gate,
                 op0=ALU.add,
                 op1=ALU.subtract,
             )
+            return lead_j
+
+        fresh = result("fresh")
+        nc.vector.tensor_tensor(out=fresh[:], in0=i_gate, in1=c_hat, op=ALU.mult)
+        kept = result("kept")
+        nc.vector.tensor_tensor(out=kept[:], in0=f_gate, in1=c_masked[:], op=ALU.mult)
+        c_t = result("c_t")
+        tanh_c = result("tanh_c")
+        for h in range(HALVES):
+            nc.vector.scalar_tensor_tensor(
+                out=c_t[:, h, :],
+                in0=fresh[:, h, :],
+                scalar=mask_col[:, h : h + 1],
+                in1=kept[:, h, :],
+                op0=ALU.mult,
+                op1=ALU.add,
+            )
+            nc.scalar.activation(out=tanh_c[:, h, :], in_=c_t[:, h, :], func=ACT.Tanh)
+        store(out_1, c_t)
+        lead_0 = lead(0)
+        lead_1 = lead(1)
         t = result("t")
         nc.vector.scalar_tensor_tensor(out=t[:], in0=tanh_c[:], scalar=0.0, in1=mask_wide, op0=ALU.add, op1=ALU.mult)
+        lead_2 = lead(2)
+        s_0 = result("s_0")
+        nc.vector.tensor_tensor(out=s_0[:], in0=lead_0[:], in1=t[:], op=ALU.mult)
+        store(out_2, s_0)
         h_out = result("h_out")
         nc.vector.tensor_tensor(out=h_out[:], in0=o_gate, in1=t[:], op=ALU.mult)
         store(out_0, h_out)
-        s_0 = result("s_0")
-        nc.vector.tensor_tensor(out=s_0[:], in0=lead[0][:], in1=t[:], op=ALU.mult)
-        store(out_2, s_0)
         rest_1 = result("rest_1")
-        nc.vector.tensor_tensor(out=rest_1[:], in0=lead[1][:], in1=s_0[:], op=ALU.subtract)
+        nc.vector.tensor_tensor(out=rest_1[:], in0=lead_1[:], in1=s_0[:], op=ALU.subtract)
+        rest_2a = result("rest_2a")
+        nc.vector.scalar_tensor_tensor(
+            out=rest_2a[:], in0=s_0[:], scalar=-2.0, in1=lead_2[:], op0=ALU.mult, op1=ALU.add
+        )
         s_1 = result("s_1")
         nc.vector.scalar_tensor_tensor(out=s_1[:], in0=rest_1[:], scalar=0.5, in1=t[:], op0=ALU.mult, op1=ALU.mult)
         store(out_3, s_1)
-        rest_2a = result("rest_2a")
-        nc.vector.scalar_tensor_tensor(
-            out=rest_2a[:], in0=s_0[:], scalar=-2.0, in1=lead[2][:], op0=ALU.mult, op1=ALU.add
-        )
         rest_2 = result("rest_2")
         nc.vector.tensor_tensor(out=rest_2[:], in0=rest_2a[:], in1=s_1[:], op=ALU.subtract)
         s_2 = result("s_2")

@@ -20,6 +20,7 @@ WORDS = K_PASS // 2
 GROUPS = 16384 // K_PASS
 N_ALL = 7 * DH
 N_LSTM = 4 * DH
+N_SHARED = 3 * DH
 
 ROUND = 2
 ROUNDS = GROUPS // ROUND
@@ -27,6 +28,9 @@ BLOCK = 4
 BLOCKS = GROUPS // BLOCK
 ROUNDS_IN_BLOCK = BLOCK // ROUND
 AHEAD = 3
+SPLIT = 6
+SPLIT_FROM = ROUNDS - SPLIT
+SHARED_LOADS = {1: ((20, 4), (24, 4), (28, 4)), 2: ((20, 4), (24, 4), (28, 2), (30, 2))}
 
 COLUMN_RANGES = ((0, 512), (512, 256), (768, 128))
 
@@ -69,6 +73,8 @@ def tile_share_lstm_cell_pa_k_kernel(
         x_pool = ctx.enter_context(tc.tile_pool(name="x_pool", bufs=AHEAD + 1))
         w_pool = ctx.enter_context(tc.tile_pool(name="w_pool", bufs=ROUNDS_IN_BLOCK * (AHEAD + 1)))
         sort_pool = ctx.enter_context(tc.tile_pool(name="sort_pool", bufs=2))
+        w_split_pool = ctx.enter_context(tc.tile_pool(name="w_split_pool", bufs=SPLIT))
+        code_split_pool = ctx.enter_context(tc.tile_pool(name="code_split_pool", bufs=SPLIT))
         quant_pool = ctx.enter_context(tc.tile_pool(name="quant_pool", bufs=3))
         acc_pool = ctx.enter_context(tc.psum_pool(name="acc_pool", bufs=1))
         flip_pool = ctx.enter_context(tc.psum_pool(name="flip_pool", bufs=ROUND))
@@ -77,6 +83,7 @@ def tile_share_lstm_cell_pa_k_kernel(
 
         x_tiles = {}
         w_tiles = {}
+        w_shared = {1: {}, 2: {}}
 
         def load_x(block):
             x_tile = x_pool.tile([P, HALVES, BLOCK * K_PASS], BF16, name="x_tile")
@@ -84,19 +91,34 @@ def tile_share_lstm_cell_pa_k_kernel(
             nc.sync.dma_start(out=x_tile[:], in_=x_rows[:, :, k_from : k_from + BLOCK * K_PASS])
             x_tiles[block] = x_tile
 
-        def load_w(rnd):
-            w_tile = w_pool.tile([P, ROUND, N_ALL], U32, name="w_tile", align_bytes=64)
+        def load_columns(pool, name, group, groups, col_from, col_to):
+            w_tile = pool.tile([P, groups, col_to - col_from], U32, name=name, align_bytes=64)
             nc.sync.dma_start(
                 out=w_tile[:].bitcast(I32),
-                in_=w_words[:, rnd * ROUND : (rnd + 1) * ROUND, :].bitcast(I32),
+                in_=w_words[:, group : group + groups, 4 * col_from : 4 * col_to].bitcast(I32),
             )
-            w_tiles[rnd] = w_tile
+            return {group + i: w_tile[:, i, :] for i in range(groups)}
+
+        def load_w(rnd):
+            if rnd < SPLIT_FROM:
+                w_tiles.update(load_columns(w_pool, "w_tile", rnd * ROUND, ROUND, 0, N_ALL))
+            else:
+                w_tiles.update(load_columns(w_split_pool, "w_lstm", rnd * ROUND, ROUND, 0, N_LSTM))
+
+        def load_shared():
+            for c, loads in SHARED_LOADS.items():
+                col_from, width = COLUMN_RANGES[c]
+                for group, groups in loads:
+                    tiles = load_columns(keep, "w_%d_%d" % (c, group), group, groups, col_from, col_from + width)
+                    w_shared[c].update(tiles)
 
         def load_block(block):
             load_w(block * ROUNDS_IN_BLOCK)
             if block + 1 < BLOCKS:
                 load_x(block + 1)
             load_w(block * ROUNDS_IN_BLOCK + 1)
+            if block + 1 == BLOCKS:
+                load_shared()
 
         acts_in = keep.tile([P, 4, HALVES, DH], BF16)
         for a, rows in enumerate((h_minors, s0, s1, s2)):
@@ -166,8 +188,9 @@ def tile_share_lstm_cell_pa_k_kernel(
                             ident_f32[:],
                         )
                 nc.scalar.copy(out=grouped_words[:, g], in_=flipped[:].rearrange("p u h b -> p (h b) u"))
-            codes = quant_pool.tile([P, ROUND * HALVES * P], U32, name="codes", align_bytes=64)
-            plane = quant_pool.tile([P, ROUND * HALVES * P], U8, name="plane", align_bytes=64)
+            pool = quant_pool if rnd < SPLIT_FROM else code_split_pool
+            codes = pool.tile([P, ROUND * HALVES * P], U32, name="codes", align_bytes=64)
+            plane = pool.tile([P, ROUND * HALVES * P], U8, name="plane", align_bytes=64)
             nc.vector.quantize_mx(out=codes[:].bitcast(FP8X4), scales=plane[:], in_=grouped[:])
             x_codes[rnd] = codes
             x_planes[rnd] = plane
@@ -209,6 +232,23 @@ def tile_share_lstm_cell_pa_k_kernel(
             for h in range(HALVES):
                 acc[c, h] = acc_pool.tile([P, width], F32, name="acc", tag="acc_%d_%d" % (c, h))
 
+        def multiply(groups, c, words, words_from):
+            col_from, width = COLUMN_RANGES[c]
+            for h in range(HALVES):
+                for group in groups:
+                    rnd, g = divmod(group, ROUND)
+                    offset = 4 * (group % BLOCK)
+                    rows = slice((g * HALVES + h) * P, (g * HALVES + h + 1) * P)
+                    nc.tensor.matmul_mx(
+                        out=acc[c, h][:],
+                        lhsT=x_codes[rnd][:, rows].bitcast(FP8X4),
+                        lhsT_scale=x_planes[rnd][:, rows],
+                        rhs=words[group][:, col_from - words_from : col_from - words_from + width].bitcast(FP8X4),
+                        rhs_scale=w_planes[offset:P, group // BLOCK, col_from : col_from + width],
+                        start=(group == 0),
+                        stop=(group == GROUPS - 1),
+                    )
+
         sort_x(0)
         flip_x(0)
         for rnd in range(ROUNDS):
@@ -219,20 +259,12 @@ def tile_share_lstm_cell_pa_k_kernel(
                 sort_x(block + 1)
             if rnd + 1 < ROUNDS:
                 flip_x(rnd + 1)
-            for c, (col_from, width) in enumerate(COLUMN_RANGES):
-                for h in range(HALVES):
-                    for g in range(ROUND):
-                        offset = 4 * (part * ROUND + g)
-                        rows = slice((g * HALVES + h) * P, (g * HALVES + h + 1) * P)
-                        nc.tensor.matmul_mx(
-                            out=acc[c, h][:],
-                            lhsT=x_codes[rnd][:, rows].bitcast(FP8X4),
-                            lhsT_scale=x_planes[rnd][:, rows],
-                            rhs=w_tiles[rnd][:, g, col_from : col_from + width].bitcast(FP8X4),
-                            rhs_scale=w_planes[offset:P, block, col_from : col_from + width],
-                            start=(rnd == 0 and g == 0),
-                            stop=(rnd == ROUNDS - 1 and g == ROUND - 1),
-                        )
+            groups = range(rnd * ROUND, (rnd + 1) * ROUND)
+            for c in range(3 if rnd < SPLIT_FROM else 1):
+                multiply(groups, c, w_tiles, 0)
+        for c, loads in SHARED_LOADS.items():
+            for group, groups in loads:
+                multiply(range(group, group + groups), c, w_shared[c], COLUMN_RANGES[c][0])
 
         def result(name):
             return keep.tile([P, HALVES, DH], F32, name=name)
@@ -248,38 +280,38 @@ def tile_share_lstm_cell_pa_k_kernel(
 
         pre = keep.tile([P, HALVES, N_ALL], F32)
         gate = keep.tile([P, HALVES, N_ALL], F32)
-        for c, (col_from, width) in enumerate(COLUMN_RANGES):
-            for h in range(HALVES):
-                cols = slice(col_from, col_from + width)
-                nc.vector.tensor_tensor(out=pre[:, h, cols], in0=acc[c, h][:], in1=addend[:, h, cols], op=ALU.add)
+
+        def add_up(c, h, col_from, col_to):
+            base = COLUMN_RANGES[c][0]
+            nc.vector.tensor_tensor(
+                out=pre[:, h, col_from:col_to],
+                in0=acc[c, h][:, col_from - base : col_to - base],
+                in1=addend[:, h, col_from:col_to],
+                op=ALU.add,
+            )
+
+        def squash(func, h, col_from, col_to):
+            nc.scalar.activation(out=gate[:, h, col_from:col_to], in_=pre[:, h, col_from:col_to], func=func)
+
         for h in range(HALVES):
-            nc.scalar.activation(out=gate[:, h, 0 : 3 * DH], in_=pre[:, h, 0 : 3 * DH], func=ACT.Sigmoid)
-            nc.scalar.activation(out=gate[:, h, 3 * DH : N_LSTM], in_=pre[:, h, 3 * DH : N_LSTM], func=ACT.Tanh)
+            add_up(0, h, 3 * DH, N_LSTM)
+            squash(ACT.Tanh, h, 3 * DH, N_LSTM)
+            add_up(0, h, 0, 2 * DH)
+            squash(ACT.Sigmoid, h, 0, 2 * DH)
         for h in range(HALVES):
-            nc.scalar.activation(out=gate[:, h, N_LSTM:N_ALL], in_=pre[:, h, N_LSTM:N_ALL], func=ACT.Sigmoid)
+            add_up(0, h, 2 * DH, 3 * DH)
+        squash(ACT.Sigmoid, slice(0, HALVES), 2 * DH, 3 * DH)
         i_gate = gate[:, :, 0:DH]
         f_gate = gate[:, :, DH : 2 * DH]
         o_gate = gate[:, :, 2 * DH : 3 * DH]
         c_hat = gate[:, :, 3 * DH : 4 * DH]
-
-        def lead(j):
-            lead_j = result("lead%d" % j)
-            nc.vector.scalar_tensor_tensor(
-                out=lead_j[:],
-                in0=gate[:, :, N_LSTM + j * DH : N_LSTM + (j + 1) * DH],
-                scalar=float(j + 1),
-                in1=o_gate,
-                op0=ALU.add,
-                op1=ALU.subtract,
-            )
-            return lead_j
-
         fresh = result("fresh")
-        nc.vector.tensor_tensor(out=fresh[:], in0=i_gate, in1=c_hat, op=ALU.mult)
         kept = result("kept")
-        nc.vector.tensor_tensor(out=kept[:], in0=f_gate, in1=c_masked[:], op=ALU.mult)
         c_t = result("c_t")
         tanh_c = result("tanh_c")
+        for h in range(HALVES):
+            nc.vector.tensor_tensor(out=kept[:, h, :], in0=f_gate[:, h, :], in1=c_masked[:, h, :], op=ALU.mult)
+            nc.vector.tensor_tensor(out=fresh[:, h, :], in0=i_gate[:, h, :], in1=c_hat[:, h, :], op=ALU.mult)
         for h in range(HALVES):
             nc.vector.scalar_tensor_tensor(
                 out=c_t[:, h, :],
@@ -291,30 +323,61 @@ def tile_share_lstm_cell_pa_k_kernel(
             )
             nc.scalar.activation(out=tanh_c[:, h, :], in_=c_t[:, h, :], func=ACT.Tanh)
         store(out_1, c_t)
-        lead_0 = lead(0)
-        lead_1 = lead(1)
+        for h in range(HALVES):
+            add_up(1, h, N_LSTM, N_LSTM + 2 * DH)
+            squash(ACT.Sigmoid, h, N_LSTM, N_LSTM + 2 * DH)
         t = result("t")
-        nc.vector.scalar_tensor_tensor(out=t[:], in0=tanh_c[:], scalar=0.0, in1=mask_wide, op0=ALU.add, op1=ALU.mult)
-        lead_2 = lead(2)
-        s_0 = result("s_0")
-        nc.vector.tensor_tensor(out=s_0[:], in0=lead_0[:], in1=t[:], op=ALU.mult)
-        store(out_2, s_0)
+        for h in range(HALVES):
+            nc.vector.tensor_scalar(
+                out=t[:, h, :],
+                in0=tanh_c[:, h, :],
+                scalar1=0.0,
+                scalar2=mask_col[:, h : h + 1],
+                op0=ALU.add,
+                op1=ALU.mult,
+            )
         h_out = result("h_out")
         nc.vector.tensor_tensor(out=h_out[:], in0=o_gate, in1=t[:], op=ALU.mult)
         store(out_0, h_out)
+
+        leads = keep.tile([P, HALVES, 2, DH], F32)
+        nc.vector.tensor_tensor(
+            out=leads[:],
+            in0=gate[:, :, N_LSTM : N_LSTM + 2 * DH].rearrange("p h (j n) -> p h j n", n=DH),
+            in1=o_gate.unsqueeze(2).to_broadcast([P, HALVES, 2, DH]),
+            op=ALU.subtract,
+        )
+        s_0 = result("s_0")
+        nc.vector.scalar_tensor_tensor(
+            out=s_0[:], in0=leads[:, :, 0, :], scalar=1.0, in1=t[:], op0=ALU.add, op1=ALU.mult
+        )
+        store(out_2, s_0)
         rest_1 = result("rest_1")
-        nc.vector.tensor_tensor(out=rest_1[:], in0=lead_1[:], in1=s_0[:], op=ALU.subtract)
+        nc.vector.scalar_tensor_tensor(
+            out=rest_1[:], in0=leads[:, :, 1, :], scalar=2.0, in1=s_0[:], op0=ALU.add, op1=ALU.subtract
+        )
         rest_2a = result("rest_2a")
         nc.vector.scalar_tensor_tensor(
-            out=rest_2a[:], in0=s_0[:], scalar=-2.0, in1=lead_2[:], op0=ALU.mult, op1=ALU.add
+            out=rest_2a[:], in0=s_0[:], scalar=-2.0, in1=o_gate, op0=ALU.mult, op1=ALU.subtract
         )
         s_1 = result("s_1")
         nc.vector.scalar_tensor_tensor(out=s_1[:], in0=rest_1[:], scalar=0.5, in1=t[:], op0=ALU.mult, op1=ALU.mult)
         store(out_3, s_1)
-        rest_2 = result("rest_2")
-        nc.vector.tensor_tensor(out=rest_2[:], in0=rest_2a[:], in1=s_1[:], op=ALU.subtract)
-        s_2 = result("s_2")
+        for h in range(HALVES):
+            add_up(2, h, N_LSTM + 2 * DH, N_ALL)
+            squash(ACT.Sigmoid, h, N_LSTM + 2 * DH, N_ALL)
+        rest_2b = result("rest_2b")
         nc.vector.scalar_tensor_tensor(
-            out=s_2[:], in0=rest_2[:], scalar=1.0 / 3.0, in1=t[:], op0=ALU.mult, op1=ALU.mult
+            out=rest_2b[:], in0=rest_2a[:], scalar=3.0, in1=s_1[:], op0=ALU.add, op1=ALU.subtract
         )
+        rest_2 = result("rest_2")
+        s_2 = result("s_2")
+        for h in range(HALVES):
+            nc.vector.tensor_tensor(
+                out=rest_2[:, h, :], in0=gate[:, h, N_LSTM + 2 * DH : N_ALL], in1=rest_2b[:, h, :], op=ALU.add
+            )
+        for h in range(HALVES):
+            nc.vector.scalar_tensor_tensor(
+                out=s_2[:, h, :], in0=rest_2[:, h, :], scalar=1.0 / 3.0, in1=t[:, h, :], op0=ALU.mult, op1=ALU.mult
+            )
         store(out_4, s_2)

@@ -81,6 +81,8 @@ def tile_share_lstm_cell_pa_k_kernel(
 
         w_planes = keep.tile([P, BLOCKS, N_ALL], U8, align_bytes=64)
 
+        nc.vector.memset(w_planes[:, 0, :].bitcast(I32), 0)
+
         x_tiles = {}
         w_tiles = {}
         w_shared = {1: {}, 2: {}}
@@ -88,15 +90,18 @@ def tile_share_lstm_cell_pa_k_kernel(
         def load_x(block):
             x_tile = x_pool.tile([P, HALVES, BLOCK * K_PASS], BF16, name="x_tile")
             k_from = block * BLOCK * K_PASS
-            nc.sync.dma_start(out=x_tile[:], in_=x_rows[:, :, k_from : k_from + BLOCK * K_PASS])
+            for h in range(HALVES):
+                nc.sync.dma_start(out=x_tile[:, h, :], in_=x_rows[:, h, k_from : k_from + BLOCK * K_PASS])
             x_tiles[block] = x_tile
 
         def load_columns(pool, name, group, groups, col_from, col_to):
             w_tile = pool.tile([P, groups, col_to - col_from], U32, name=name, align_bytes=64)
-            nc.sync.dma_start(
-                out=w_tile[:].bitcast(I32),
-                in_=w_words[:, group : group + groups, 4 * col_from : 4 * col_to].bitcast(I32),
-            )
+            step = groups if col_to - col_from < N_LSTM else 1
+            for i in range(0, groups, step):
+                nc.sync.dma_start(
+                    out=w_tile[:, i : i + step, :].bitcast(I32),
+                    in_=w_words[:, group + i : group + i + step, 4 * col_from : 4 * col_to].bitcast(I32),
+                )
             return {group + i: w_tile[:, i, :] for i in range(groups)}
 
         def load_w(rnd):
@@ -136,7 +141,6 @@ def tile_share_lstm_cell_pa_k_kernel(
             nc.sync.dma_start(
                 out=bias_rows[1:2, N_LSTM + j * DH : N_LSTM + (j + 1) * DH], in_=row.unsqueeze(0)
             )
-        nc.vector.memset(w_planes[:].bitcast(I32), 0)
         for block in range(AHEAD):
             load_block(block)
         c_in = keep.tile([P, HALVES, DH], BF16)
@@ -144,12 +148,13 @@ def tile_share_lstm_cell_pa_k_kernel(
         mask_in = keep.tile([P, HALVES], BF16)
         nc.sync.dma_start(out=mask_in[:], in_=mask.rearrange("(p h) -> p h", h=HALVES))
 
-        ident_bf16 = keep.tile([P, P], BF16)
-        make_identity(nc, ident_bf16[:])
         ident_f32 = keep.tile([P, P], F32)
         make_identity(nc, ident_f32[:])
+        ident_bf16 = keep.tile([P, P], BF16)
+        nc.vector.tensor_copy(out=ident_bf16[:], in_=ident_f32[:])
         ones = keep.tile([P, P], BF16)
-        nc.gpsimd.memset(ones[:], 1.0)
+        nc.vector.memset(ones[:], 1.0)
+        nc.vector.memset(w_planes[:, 1:BLOCKS, :].rearrange("p b n -> p (b n)").bitcast(I32), 0)
         for block in range(BLOCKS):
             for quadrant in range(4):
                 nc.gpsimd.dma_start(

from contextlib import ExitStack

import concourse.mybir as mybir
from concourse.masks import make_identity

F32 = mybir.dt.float32
BF16 = mybir.dt.bfloat16
I32 = mybir.dt.int32
U32 = mybir.dt.uint32
U8 = mybir.dt.uint8
FP8X4 = mybir.dt.float8_e4m3fn_x4
ALU = mybir.AluOpType
ACT = mybir.ActivationFunctionType

P = 128
HALVES = 2
DH = 128
K_PASS = 512
WORDS = K_PASS // 2
GROUPS = 16384 // K_PASS
N_ALL = 7 * DH
N_LSTM = 4 * DH
N_SHARED = 3 * DH

ROUND = 2
ROUNDS = GROUPS // ROUND
BLOCK = 4
BLOCKS = GROUPS // BLOCK
ROUNDS_IN_BLOCK = BLOCK // ROUND
AHEAD = 3
SPLIT = 6
SPLIT_FROM = ROUNDS - SPLIT
SHARED_LOADS = {1: ((20, 4), (24, 4), (28, 4)), 2: ((20, 4), (24, 4), (28, 2), (30, 2))}

COLUMN_RANGES = ((0, 512), (512, 256), (768, 128))

FLOPS = 2 * 256 * 16384 * N_ALL + 2 * 256 * DH * N_ALL


def tile_share_lstm_cell_pa_k_kernel(
    tc,
    x,
    h_minors,
    c_minors,
    s0,
    s1,
    s2,
    mask,
    weight_ih_words,
    weight_ih_scales,
    bias_ih,
    weight_hh,
    bias_hh,
    weight_sh0,
    bias_sh0,
    weight_sh1,
    bias_sh1,
    weight_sh2,
    bias_sh2,
    out_0,
    out_1,
    out_2,
    out_3,
    out_4,
):
    nc = tc.nc
    x_rows = x.rearrange("(p h) k -> p h k", h=HALVES)
    w_words = weight_ih_words.rearrange("g p n t -> p g (n t)")

    with ExitStack() as ctx:
        ctx.enter_context(tc.manual_schedule())
        keep = ctx.enter_context(tc.tile_pool(name="keep", bufs=1))
        x_pool = ctx.enter_context(tc.tile_pool(name="x_pool", bufs=AHEAD + 1))
        w_pool = ctx.enter_context(tc.tile_pool(name="w_pool", bufs=ROUNDS_IN_BLOCK * (AHEAD + 1)))
        sort_pool = ctx.enter_context(tc.tile_pool(name="sort_pool", bufs=2))
        w_split_pool = ctx.enter_context(tc.tile_pool(name="w_split_pool", bufs=SPLIT))
        code_split_pool = ctx.enter_context(tc.tile_pool(name="code_split_pool", bufs=SPLIT))
        quant_pool = ctx.enter_context(tc.tile_pool(name="quant_pool", bufs=3))
        acc_pool = ctx.enter_context(tc.psum_pool(name="acc_pool", bufs=1))
        flip_pool = ctx.enter_context(tc.psum_pool(name="flip_pool", bufs=ROUND))

        w_planes = keep.tile([P, BLOCKS, N_ALL], U8, align_bytes=64)

        nc.vector.memset(w_planes[:, 0, :].bitcast(I32), 0)

        x_tiles = {}
        w_tiles = {}
        w_shared = {1: {}, 2: {}}

        def load_x(block):
            x_tile = x_pool.tile([P, HALVES, BLOCK * K_PASS], BF16, name="x_tile")
            k_from = block * BLOCK * K_PASS
            for h in range(HALVES):
                nc.sync.dma_start(out=x_tile[:, h, :], in_=x_rows[:, h, k_from : k_from + BLOCK * K_PASS])
            x_tiles[block] = x_tile

        def load_columns(pool, name, group, groups, col_from, col_to):
            w_tile = pool.tile([P, groups, col_to - col_from], U32, name=name, align_bytes=64)
            step = groups if col_to - col_from < N_LSTM else 1
            for i in range(0, groups, step):
                nc.sync.dma_start(
                    out=w_tile[:, i : i + step, :].bitcast(I32),
                    in_=w_words[:, group + i : group + i + step, 4 * col_from : 4 * col_to].bitcast(I32),
                )
            return {group + i: w_tile[:, i, :] for i in range(groups)}

        def load_w(rnd):
            if rnd < SPLIT_FROM:
                w_tiles.update(load_columns(w_pool, "w_tile", rnd * ROUND, ROUND, 0, N_ALL))
            else:
                w_tiles.update(load_columns(w_split_pool, "w_lstm", rnd * ROUND, ROUND, 0, N_LSTM))

        def load_shared():
            for c, loads in SHARED_LOADS.items():
                col_from, width = COLUMN_RANGES[c]
                for group, groups in loads:
                    tiles = load_columns(keep, "w_%d_%d" % (c, group), group, groups, col_from, col_from + width)
                    w_shared[c].update(tiles)

        def load_block(block):
            load_w(block * ROUNDS_IN_BLOCK)
            if block + 1 < BLOCKS:
                load_x(block + 1)
            load_w(block * ROUNDS_IN_BLOCK + 1)
            if block + 1 == BLOCKS:
                load_shared()

        acts_in = keep.tile([P, 4, HALVES, DH], BF16)
        for a, rows in enumerate((h_minors, s0, s1, s2)):
            nc.sync.dma_start(out=acts_in[:, a], in_=rows.rearrange("(p h) k -> p h k", h=HALVES))
        wts_in = keep.tile([P, 7, DH], BF16)
        nc.sync.dma_start(out=wts_in[:, 0:4, :], in_=weight_hh.rearrange("(j n) k -> n j k", j=4))
        bias_rows = keep.tile([P, N_ALL], BF16)
        nc.vector.memset(bias_rows[:], 0.0)
        nc.sync.dma_start(out=bias_rows[0:1, :], in_=bias_ih.unsqueeze(0))
        nc.sync.dma_start(out=bias_rows[1:2, 0:N_LSTM], in_=bias_hh.unsqueeze(0))
        load_x(0)
        for j, rows in enumerate((weight_sh0, weight_sh1, weight_sh2)):
            nc.sync.dma_start(out=wts_in[:, 4 + j, :], in_=rows)
        for j, row in enumerate((bias_sh0, bias_sh1, bias_sh2)):
            nc.sync.dma_start(
                out=bias_rows[1:2, N_LSTM + j * DH : N_LSTM + (j + 1) * DH], in_=row.unsqueeze(0)
            )
        for block in range(AHEAD):
            load_block(block)
        c_in = keep.tile([P, HALVES, DH], BF16)
        nc.sync.dma_start(out=c_in[:], in_=c_minors.rearrange("(p h) k -> p h k", h=HALVES))
        mask_in = keep.tile([P, HALVES], BF16)
        nc.sync.dma_start(out=mask_in[:], in_=mask.rearrange("(p h) -> p h", h=HALVES))

        ident_f32 = keep.tile([P, P], F32)
        make_identity(nc, ident_f32[:])
        ident_bf16 = keep.tile([P, P], BF16)
        nc.vector.tensor_copy(out=ident_bf16[:], in_=ident_f32[:])
        ones = keep.tile([P, P], BF16)
        nc.vector.memset(ones[:], 1.0)
        nc.vector.memset(w_planes[:, 1:BLOCKS, :].rearrange("p b n -> p (b n)").bitcast(I32), 0)
        for block in range(BLOCKS):
            for quadrant in range(4):
                nc.gpsimd.dma_start(
                    out=w_planes[32 * quadrant : 32 * quadrant + 16, block, :].bitcast(F32),
                    in_=weight_ih_scales[
                        block * BLOCK : (block + 1) * BLOCK, 4 * quadrant : 4 * quadrant + 4, :
                    ].bitcast(F32),
                )
        warm = keep.tile([P, 1], F32)
        nc.vector.memset(warm[:], 0.0)
        nc.scalar.activation(out=warm[:], in_=warm[:], func=ACT.Sigmoid)

        sorted_blocks = {}
        x_codes = {}
        x_planes = {}

        def sort_x(block):
            sorted_block = sort_pool.tile([P, HALVES, BLOCK, 2, P], F32, name="sorted_block")
            nc.vector.tensor_copy(
                out=sorted_block[:],
                in_=x_tiles[block][:].bitcast(F32).rearrange("p h (g w u) -> p h g u w", g=BLOCK, u=2),
            )
            sorted_blocks[block] = sorted_block

        def flip_x(rnd):
            block, part = divmod(rnd, ROUNDS_IN_BLOCK)
            grouped = quant_pool.tile([P, ROUND * HALVES * P * 4], BF16, name="grouped", align_bytes=64)
            grouped_words = grouped[:].bitcast(F32).rearrange("p (g c u) -> p g c u", g=ROUND, u=2)
            for g in range(ROUND):
                flipped = flip_pool.tile([P, 2, HALVES, P], F32, name="flipped")
                for u in range(2):
                    for h in range(HALVES):
                        nc.tensor.transpose(
                            flipped[:, u, h, :],
                            sorted_blocks[block][:, h, part * ROUND + g, u, :],
                            ident_f32[:],
                        )
                nc.scalar.copy(out=grouped_words[:, g], in_=flipped[:].rearrange("p u h b -> p (h b) u"))
            pool = quant_pool if rnd < SPLIT_FROM else code_split_pool
            codes = pool.tile([P, ROUND * HALVES * P], U32, name="codes", align_bytes=64)
            plane = pool.tile([P, ROUND * HALVES * P], U8, name="plane", align_bytes=64)
            nc.vector.quantize_mx(out=codes[:].bitcast(FP8X4), scales=plane[:], in_=grouped[:])
            x_codes[rnd] = codes
            x_planes[rnd] = plane

        acts_flip = acc_pool.tile([P, 4 * HALVES, P], BF16, tag="acc_2_0")
        for a in range(4):
            for h in range(HALVES):
                nc.tensor.transpose(acts_flip[:, a * HALVES + h, :], acts_in[:, a, h, :], ident_bf16[:])
        acts_t = keep.tile([P, 4 * HALVES, P], BF16)
        nc.scalar.copy(out=acts_t[:], in_=acts_flip[:])
        wts_flip = acc_pool.tile([P, 7, P], BF16, tag="acc_2_1")
        wts_t = keep.tile([P, N_ALL], BF16)
        for j in range(4):
            nc.tensor.transpose(wts_flip[:, j, :], wts_in[:, j, :], ident_bf16[:])
        nc.scalar.copy(out=wts_t[:, 0:N_LSTM], in_=wts_flip[:, 0:4, :].rearrange("p j n -> p (j n)"))

        addend = keep.tile([P, HALVES, N_ALL], F32)
        for h in range(HALVES):
            lstm_sum = acc_pool.tile([P, N_LSTM], F32, tag="acc_0_%d" % h)
            nc.tensor.matmul(lstm_sum[:], lhsT=ones[:], rhs=bias_rows[:, 0:N_LSTM], start=True, stop=False)
            nc.tensor.matmul(lstm_sum[:], lhsT=acts_t[:, h, :], rhs=wts_t[:, 0:N_LSTM], start=False, stop=True)
            nc.scalar.copy(out=addend[:, h, 0:N_LSTM], in_=lstm_sum[:])
        for j in range(4, 7):
            nc.tensor.transpose(wts_flip[:, j, :], wts_in[:, j, :], ident_bf16[:])
        nc.scalar.copy(out=wts_t[:, N_LSTM:N_ALL], in_=wts_flip[:, 4:7, :].rearrange("p j n -> p (j n)"))
        for h in range(HALVES):
            shared_sum = acc_pool.tile([P, 3 * DH], F32, tag="acc_1_%d" % h)
            for j in range(3):
                cols = slice(N_LSTM + j * DH, N_LSTM + (j + 1) * DH)
                part_sum = shared_sum[:, j * DH : (j + 1) * DH]
                nc.tensor.matmul(part_sum, lhsT=ones[:], rhs=bias_rows[:, cols], start=True, stop=False)
                nc.tensor.matmul(
                    part_sum, lhsT=acts_t[:, (1 + j) * HALVES + h, :], rhs=wts_t[:, cols], start=False, stop=True
                )
            nc.scalar.copy(out=addend[:, h, N_LSTM:N_ALL], in_=shared_sum[:])

        acc = {}
        for c, (col_from, width) in enumerate(COLUMN_RANGES):
            for h in range(HALVES):
                acc[c, h] = acc_pool.tile([P, width], F32, name="acc", tag="acc_%d_%d" % (c, h))

        def multiply(groups, c, words, words_from):
            col_from, width = COLUMN_RANGES[c]
            for h in range(HALVES):
                for group in groups:
                    rnd, g = divmod(group, ROUND)
                    offset = 4 * (group % BLOCK)
                    rows = slice((g * HALVES + h) * P, (g * HALVES + h + 1) * P)
                    nc.tensor.matmul_mx(
                        out=acc[c, h][:],
                        lhsT=x_codes[rnd][:, rows].bitcast(FP8X4),
                        lhsT_scale=x_planes[rnd][:, rows],
                        rhs=words[group][:, col_from - words_from : col_from - words_from + width].bitcast(FP8X4),
                        rhs_scale=w_planes[offset:P, group // BLOCK, col_from : col_from + width],
                        start=(group == 0),
                        stop=(group == GROUPS - 1),
                    )

        sort_x(0)
        flip_x(0)
        for rnd in range(ROUNDS):
            block, part = divmod(rnd, ROUNDS_IN_BLOCK)
            if part == 0 and block + AHEAD < BLOCKS:
                load_block(block + AHEAD)
            if part == 0 and block + 1 < BLOCKS:
                sort_x(block + 1)
            if rnd + 1 < ROUNDS:
                flip_x(rnd + 1)
            groups = range(rnd * ROUND, (rnd + 1) * ROUND)
            for c in range(3 if rnd < SPLIT_FROM else 1):
                multiply(groups, c, w_tiles, 0)
        for c, loads in SHARED_LOADS.items():
            for group, groups in loads:
                multiply(range(group, group + groups), c, w_shared[c], COLUMN_RANGES[c][0])

        def result(name):
            return keep.tile([P, HALVES, DH], F32, name=name)

        def store(out, tile):
            nc.sync.dma_start(out=out.rearrange("(p h) n -> p h n", h=HALVES), in_=tile[:])

        mask_col = keep.tile([P, HALVES], F32)
        nc.scalar.copy(out=mask_col[:], in_=mask_in[:])
        mask_wide = mask_col[:].unsqueeze(2).to_broadcast([P, HALVES, DH])
        c_masked = result("c_masked")
        nc.vector.tensor_tensor(out=c_masked[:], in0=c_in[:], in1=mask_wide, op=ALU.mult)

        pre = keep.tile([P, HALVES, N_ALL], F32)
        gate = keep.tile([P, HALVES, N_ALL], F32)

        def add_up(c, h, col_from, col_to):
            base = COLUMN_RANGES[c][0]
            nc.vector.tensor_tensor(
                out=pre[:, h, col_from:col_to],
                in0=acc[c, h][:, col_from - base : col_to - base],
                in1=addend[:, h, col_from:col_to],
                op=ALU.add,
            )

        def squash(func, h, col_from, col_to):
            nc.scalar.activation(out=gate[:, h, col_from:col_to], in_=pre[:, h, col_from:col_to], func=func)

        for h in range(HALVES):
            add_up(0, h, 3 * DH, N_LSTM)
            squash(ACT.Tanh, h, 3 * DH, N_LSTM)
            add_up(0, h, 0, 2 * DH)
            squash(ACT.Sigmoid, h, 0, 2 * DH)
        for h in range(HALVES):
            add_up(0, h, 2 * DH, 3 * DH)
        squash(ACT.Sigmoid, slice(0, HALVES), 2 * DH, 3 * DH)
        i_gate = gate[:, :, 0:DH]
        f_gate = gate[:, :, DH : 2 * DH]
        o_gate = gate[:, :, 2 * DH : 3 * DH]
        c_hat = gate[:, :, 3 * DH : 4 * DH]
        fresh = result("fresh")
        kept = result("kept")
        c_t = result("c_t")
        tanh_c = result("tanh_c")
        for h in range(HALVES):
            nc.vector.tensor_tensor(out=kept[:, h, :], in0=f_gate[:, h, :], in1=c_masked[:, h, :], op=ALU.mult)
            nc.vector.tensor_tensor(out=fresh[:, h, :], in0=i_gate[:, h, :], in1=c_hat[:, h, :], op=ALU.mult)
        for h in range(HALVES):
            nc.vector.scalar_tensor_tensor(
                out=c_t[:, h, :],
                in0=fresh[:, h, :],
                scalar=mask_col[:, h : h + 1],
                in1=kept[:, h, :],
                op0=ALU.mult,
                op1=ALU.add,
            )
            nc.scalar.activation(out=tanh_c[:, h, :], in_=c_t[:, h, :], func=ACT.Tanh)
        store(out_1, c_t)
        for h in range(HALVES):
            add_up(1, h, N_LSTM, N_LSTM + 2 * DH)
            squash(ACT.Sigmoid, h, N_LSTM, N_LSTM + 2 * DH)
        t = result("t")
        for h in range(HALVES):
            nc.vector.tensor_scalar(
                out=t[:, h, :],
                in0=tanh_c[:, h, :],
                scalar1=0.0,
                scalar2=mask_col[:, h : h + 1],
                op0=ALU.add,
                op1=ALU.mult,
            )
        h_out = result("h_out")
        nc.vector.tensor_tensor(out=h_out[:], in0=o_gate, in1=t[:], op=ALU.mult)
        store(out_0, h_out)

        leads = keep.tile([P, HALVES, 2, DH], F32)
        nc.vector.tensor_tensor(
            out=leads[:],
            in0=gate[:, :, N_LSTM : N_LSTM + 2 * DH].rearrange("p h (j n) -> p h j n", n=DH),
            in1=o_gate.unsqueeze(2).to_broadcast([P, HALVES, 2, DH]),
            op=ALU.subtract,
        )
        s_0 = result("s_0")
        nc.vector.scalar_tensor_tensor(
            out=s_0[:], in0=leads[:, :, 0, :], scalar=1.0, in1=t[:], op0=ALU.add, op1=ALU.mult
        )
        store(out_2, s_0)
        rest_1 = result("rest_1")
        nc.vector.scalar_tensor_tensor(
            out=rest_1[:], in0=leads[:, :, 1, :], scalar=2.0, in1=s_0[:], op0=ALU.add, op1=ALU.subtract
        )
        rest_2a = result("rest_2a")
        nc.vector.scalar_tensor_tensor(
            out=rest_2a[:], in0=s_0[:], scalar=-2.0, in1=o_gate, op0=ALU.mult, op1=ALU.subtract
        )
        s_1 = result("s_1")
        nc.vector.scalar_tensor_tensor(out=s_1[:], in0=rest_1[:], scalar=0.5, in1=t[:], op0=ALU.mult, op1=ALU.mult)
        store(out_3, s_1)
        for h in range(HALVES):
            add_up(2, h, N_LSTM + 2 * DH, N_ALL)
            squash(ACT.Sigmoid, h, N_LSTM + 2 * DH, N_ALL)
        rest_2b = result("rest_2b")
        nc.vector.scalar_tensor_tensor(
            out=rest_2b[:], in0=rest_2a[:], scalar=3.0, in1=s_1[:], op0=ALU.add, op1=ALU.subtract
        )
        rest_2 = result("rest_2")
        s_2 = result("s_2")
        for h in range(HALVES):
            nc.vector.tensor_tensor(
                out=rest_2[:, h, :], in0=gate[:, h, N_LSTM + 2 * DH : N_ALL], in1=rest_2b[:, h, :], op=ALU.add
            )
        for h in range(HALVES):
            nc.vector.scalar_tensor_tensor(
                out=s_2[:, h, :], in0=rest_2[:, h, :], scalar=1.0 / 3.0, in1=t[:, h, :], op0=ALU.mult, op1=ALU.mult
            )
        store(out_4, s_2)
